import numpy as np
import ml_dtypes


def mxq(x, axis, fmt="e4m3"):
    dtype, down = {"e4m3": (ml_dtypes.float8_e4m3fn, 7), "e5m2": (ml_dtypes.float8_e5m2, 14)}[fmt]
    v = np.moveaxis(np.asarray(x, np.float32).astype(ml_dtypes.bfloat16).astype(np.float64), axis, -1)
    blocks = v.reshape(v.shape[:-1] + (-1, 32))
    amax = np.abs(blocks).max(-1, keepdims=True)
    byte = np.maximum(np.where(amax > 0, np.frexp(amax)[1] - 1 + 127, 0) - down, 1)
    scale = np.exp2(byte - 127.0)
    codes = (blocks / scale).astype(np.float32).astype(dtype).astype(np.float64)
    return np.moveaxis((codes * scale).reshape(v.shape), -1, axis)


WIDE = False


def mx_kscale(k):
    if not WIDE:
        return np.ones(k)
    levels = np.array([18, -18])
    if k % 512:
        return np.exp2(np.random.permutation(np.resize(levels, k // 32))).repeat(32)
    a = np.empty((k // 512, 16))
    for p in range(k // 512):
        a[p, :8] = np.random.permutation(np.resize(levels, 8))
        for g in range(8):
            far = levels[np.abs(levels - a[p, g]) >= 10]
            a[p, g + 8] = far[np.random.randint(len(far))]
    return np.exp2(a.ravel()).repeat(32)


BF16 = ml_dtypes.bfloat16


def bf(x):
    return np.asarray(x, np.float32).astype(BF16)


def f64(x):
    return np.asarray(x).astype(np.float64)


I, M, O, B = 1024, 1024, 1024, 1024


def sigmoid(v):
    return 1.0 / (1.0 + np.exp(-v))


def setup_inputs():
    u = mx_kscale(O)
    v = mx_kscale(M)
    s = mx_kscale(B)
    x0 = bf(np.random.standard_normal((I, B)))
    out0 = bf(np.tanh(np.random.standard_normal((O, B))))
    mem0 = bf(np.random.standard_normal((M, B)) * 0.8)
    inp_out = bf(sigmoid(np.random.standard_normal((M, B)) * 1.2) * sigmoid(np.random.standard_normal((M, B)) * 1.4))
    w_readgate0 = bf(np.random.standard_normal((M, I)) / np.sqrt(I))
    w_rec_readgate = bf(np.random.standard_normal((M, O)) / np.sqrt(O))
    w_mem_readgate = bf(np.random.standard_normal((M, M)) / np.sqrt(M))
    w_hid_out0 = bf(np.random.standard_normal((O, M)) / np.sqrt(M))
    g = bf(np.random.standard_normal((O, B)) * np.exp2(np.random.randint(-6, 1, (1, B))) * 8.0 * u[:, None] / s[None, :])
    mem_out = sigmoid(f64(w_readgate0) @ f64(x0) + f64(w_rec_readgate) @ f64(out0) + f64(w_mem_readgate) @ f64(mem0))
    y = np.tanh(f64(w_hid_out0) @ (mem_out + f64(inp_out)))
    return {
        "x": bf(f64(x0) * s[None, :]),
        "out0": out0,
        "mem0": mem0,
        "inp_out": inp_out,
        "w_readgate": bf(f64(w_readgate0) / v[:, None]),
        "w_rec_readgate": w_rec_readgate,
        "w_mem_readgate": w_mem_readgate,
        "w_hid_out": bf(f64(w_hid_out0) * v[None, :] / u[:, None]),
        "mem_out": np.asarray(mem_out, np.float32),
        "y": np.asarray(y, np.float32),
        "grad_out": g,
    }


def reference(x, out0, mem0, inp_out, w_readgate, w_rec_readgate, w_mem_readgate, w_hid_out, mem_out, y, grad_out):
    m = f64(mem_out)
    yf = f64(y)
    dz2 = f64(grad_out) * (1.0 - yf * yf)
    dh = mxq(f64(w_hid_out), 0, "e4m3").T @ mxq(dz2, 0, "e5m2")
    dz1 = dh * (m * (1.0 - m))
    dx = mxq(f64(w_readgate), 0, "e4m3").T @ mxq(dz1, 0, "e5m2")
    dw = mxq(dz1, 1, "e5m2") @ mxq(f64(x), 1, "e4m3").T
    return dx, dw

@@ -1,0 +1,321 @@
+from contextlib import ExitStack
+
+import concourse.mybir as mybir
+from concourse.masks import make_identity
+
+F32 = mybir.dt.float32
+BF16 = mybir.dt.bfloat16
+U32 = mybir.dt.uint32
+U8 = mybir.dt.uint8
+E4M3 = mybir.dt.float8_e4m3fn_x4
+E5M2 = mybir.dt.float8_e5m2_x4
+ACT = mybir.ActivationFunctionType
+ALU = mybir.AluOpType
+
+SIZE = 1024
+P = 128
+PACK = 4
+HALF = 512
+
+FLOPS = 3 * 2 * SIZE * SIZE * SIZE
+BYTES = 4 * SIZE * SIZE * 2 + 2 * SIZE * SIZE * 4 + 2 * SIZE * SIZE * 4
+
+
+def tile_pt_grumb_pb_v_kernel(
+    tc, x, out0, mem0, inp_out, w_readgate, w_rec_readgate, w_mem_readgate, w_hid_out, mem_out, y, grad_out, out_0, out_1
+):
+    nc = tc.nc
+    w_hid_hbm = w_hid_out.rearrange("(k p j) m -> k p j m", p=P, j=PACK)
+    w_rg_hbm = w_readgate.rearrange("(k p j) i -> k p j i", p=P, j=PACK)
+    y_hbm = y.rearrange("(k p j) b -> k p j b", p=P, j=PACK)
+    grad_hbm = grad_out.rearrange("(k p j) b -> k p j b", p=P, j=PACK)
+    mem_hbm = mem_out.rearrange("(g p t) b -> g p t b", p=P, t=PACK)
+    x_hbm = x.rearrange("(n a p) b -> n p a b", p=P, a=4)
+    out_0_hbm = out_0.rearrange("(z a p) b -> z p a b", p=P, a=2)
+    out_1_hbm = out_1.rearrange("(g p t) i -> g p t i", p=P, t=PACK)
+
+    with ExitStack() as ctx:
+        keep = ctx.enter_context(tc.tile_pool(name="keep", bufs=1))
+        raw = ctx.enter_context(tc.tile_pool(name="raw", bufs=1))
+        work = ctx.enter_context(tc.tile_pool(name="work", bufs=6))
+        psum = ctx.enter_context(tc.psum_pool(name="psum", bufs=8))
+
+        def keep_tile(shape, dtype, name):
+            return keep.tile(shape, dtype, name=name, tag=name, align_bytes=64)
+
+        def codes_pair(name):
+            codes = keep_tile([P, 2, SIZE], U32, name + "_codes")
+            scales = keep_tile([P, 2, SIZE], U8, name + "_scales")
+            return codes, scales
+
+        w_hid_q = codes_pair("w_hid")
+        w_rg_q = codes_pair("w_rg")
+        dz2_q = codes_pair("dz2")
+        dz1_q = codes_pair("dz1")
+        dz1_t_q = codes_pair("dz1_t")
+        x_t_q = codes_pair("x_t")
+        dz1 = [keep_tile([P, PACK, SIZE], BF16, "dz1_%d" % g) for g in range(2)]
+        ident_f32 = keep_tile([P, P], F32, "ident_f32")
+        minus_half = keep_tile([P, 1], F32, "minus_half")
+
+        def bank(shape, dtype):
+            return psum.tile(shape, dtype, name="bank", tag="bank")
+
+        def grouped_tile():
+            return work.tile([P, HALF, PACK], BF16, name="grouped", tag="grouped", align_bytes=64, bufs=6)
+
+        def half(n):
+            return slice(n * HALF, (n + 1) * HALF)
+
+        def move(engine, out, in_):
+            if engine == "S":
+                nc.scalar.copy(out=out, in_=in_)
+            else:
+                nc.vector.tensor_copy(out=out, in_=in_)
+
+        def quantize(pair, dtype, row, cols, grouped):
+            codes, scales = pair
+            nc.vector.quantize_mx(
+                out=codes[:, row, cols].bitcast(dtype),
+                scales=scales[:, row, cols],
+                in_=grouped[:].rearrange("p n j -> p (n j)"),
+            )
+
+        def product(out, lhs, lhs_dtype, lhs_cols, rhs, rhs_dtype, rhs_cols):
+            for k in range(2):
+                nc.tensor.matmul_mx(
+                    out=out,
+                    lhsT=lhs[0][:, k, lhs_cols].bitcast(lhs_dtype),
+                    lhsT_scale=lhs[1][:, k, lhs_cols],
+                    rhs=rhs[0][:, k, rhs_cols].bitcast(rhs_dtype),
+                    rhs_scale=rhs[1][:, k, rhs_cols],
+                    start=(k == 0),
+                    stop=(k == 1),
+                )
+
+        def load_w(hbm, k, name, pieces=(slice(0, SIZE),)):
+            t = raw.tile([P, PACK, SIZE], BF16, name=name, tag="w_raw", align_bytes=64, bufs=3)
+            for cols in pieces:
+                nc.sync.dma_start(out=t[:, :, cols], in_=hbm[k][:, :, cols])
+            return t
+
+        def load_f32(hbm, k, h, name):
+            t = raw.tile([P, PACK, HALF], F32, name=name, tag="f32_raw", align_bytes=64, bufs=5)
+            nc.sync.dma_start(out=t[:], in_=hbm[k][:, :, half(h)])
+            return t
+
+        y_raw, mem_raw, w_hid_raw, w_rg_raw, grad_raw, x_raw = {}, {}, {}, {}, {}, {}
+
+        def load_grad(k, h):
+            t = raw.tile([P, PACK, HALF], BF16, name="grad_raw", tag="grad_raw", align_bytes=64, bufs=4)
+            nc.sync.dma_start(out=t[:], in_=grad_hbm[k][:, :, half(h)])
+            grad_raw[k, h] = t
+
+        def load_x(n):
+            t = raw.tile([P, 4, SIZE], BF16, name="x_raw", tag="x_raw", align_bytes=64, bufs=2)
+            nc.sync.dma_start(out=t[:], in_=x_hbm[n])
+            x_raw[n] = t
+
+        y_squared = {}
+
+        def square_y(k, h):
+            t = work.tile([P, HALF, PACK], F32, name="y_squared", tag="y_squared", align_bytes=64, bufs=2)
+            nc.scalar.activation(
+                out=t[:].rearrange("p (c i) j -> p c j i", i=4),
+                in_=y_raw[k, h][:].rearrange("p j (c i) -> p c j i", i=4),
+                func=ACT.Square,
+            )
+            y_squared[k, h] = t
+
+        def square_mem(g, h):
+            t = mem_raw[g, h]
+            nc.scalar.activation(out=t[:], in_=t[:], func=ACT.Square, bias=minus_half[:])
+
+        dz2_grouped = {}
+
+        def make_dz2(k, h):
+            grouped = grouped_tile()
+            nc.vector.scalar_tensor_tensor(
+                out=grouped[:],
+                in0=y_squared[k, h][:],
+                scalar=1.0,
+                in1=grad_raw[k, h][:].rearrange("p j b -> p b j"),
+                op0=ALU.subtract,
+                op1=ALU.mult,
+            )
+            dz2_grouped[k, h] = grouped
+
+        def quantize_dz2(k, h):
+            quantize(dz2_q, E5M2, k, half(h), dz2_grouped[k, h])
+
+        w_grouped = {}
+
+        def interleave_w(raw_tile, key, c, permuted, engine):
+            cols = raw_tile[:, :, half(c)]
+            grouped = grouped_tile()
+            if permuted:
+                move(engine, grouped[:].rearrange("p (t m) j -> p t m j", t=PACK), cols.rearrange("p j (m t) -> p t m j", t=PACK))
+            else:
+                move(
+                    engine,
+                    grouped[:].rearrange("p (c i) j -> p c j i", i=4),
+                    cols.rearrange("p j (c i) -> p c j i", i=4),
+                )
+            w_grouped[key, c] = grouped
+
+        def hidden_products(g, h):
+            dh = []
+            for t in range(PACK):
+                ps = bank([P, HALF], F32)
+                first = g * HALF + t * P
+                product(ps[:], w_hid_q, E4M3, slice(first, first + P), dz2_q, E5M2, half(h))
+                dh.append(ps)
+            return dh
+
+        def make_dz1(g, h, dh):
+            for t in range(PACK):
+                nc.vector.scalar_tensor_tensor(
+                    out=dz1[g][:, t, half(h)],
+                    in0=mem_raw[g, h][:, t, :],
+                    scalar=0.25,
+                    in1=dh[t][:],
+                    op0=ALU.subtract,
+                    op1=ALU.mult,
+                )
+
+        def transposed_group(source, h, engines):
+            words = source[:].rearrange("p a b -> p (a b)").bitcast(F32)
+            grouped = grouped_tile()
+            target = grouped[:].rearrange("p n j -> p (n j)").bitcast(F32)
+            for z in range(2):
+                ps = bank([P, 2, 2, P], F32)
+                for a in range(2):
+                    for u in range(2):
+                        first = (2 * z + a) * HALF + h * 2 * P + u
+                        nc.tensor.transpose(ps[:, a, u, :], words[:, first : first + 2 * P - 1 : 2], ident_f32[:])
+                move(
+                    engines[z],
+                    target[:, z * HALF : (z + 1) * HALF].rearrange("p (a r u) -> p a r u", a=2, u=2),
+                    ps[:].rearrange("p a u r -> p a r u"),
+                )
+            return grouped
+
+        def interleave_dz1(g, h, engine):
+            grouped = grouped_tile()
+            move(
+                engine,
+                grouped[:].rearrange("p (c i) t -> p c t i", i=4),
+                dz1[g][:, :, half(h)].rearrange("p t (c i) -> p c t i", i=4),
+            )
+            return grouped
+
+        def out_0_tiles(h, z, engines):
+            stage = work.tile([P, 2, HALF], F32, name="stage", tag="stage", align_bytes=64, bufs=5)
+            for a in range(2):
+                ps = bank([P, HALF], F32)
+                first = (2 * z + a) * P
+                product(ps[:], w_rg_q, E4M3, slice(first, first + P), dz1_q, E5M2, half(h))
+                move(engines[a], stage[:, a, :], ps[:])
+            nc.sync.dma_start(out=out_0_hbm[z][:, :, half(h)], in_=stage[:])
+
+        def out_1_tiles(g, z, n, engines):
+            stage = work.tile([P, 2, HALF], F32, name="stage", tag="stage", align_bytes=64, bufs=5)
+            for a in range(2):
+                ps = bank([P, HALF], F32)
+                first = g * HALF + (2 * z + a) * P
+                product(ps[:], dz1_t_q, E5M2, slice(first, first + P), x_t_q, E4M3, half(n))
+                move(engines[a], stage[:, a, :], ps[:])
+            nc.sync.dma_start(out=out_1_hbm[g][:, 2 * z : 2 * z + 2, half(n)], in_=stage[:])
+
+        nc.vector.memset(minus_half[:], -0.5)
+        make_identity(nc, ident_f32[:])
+
+        with tc.manual_schedule():
+            w_hid_raw[0] = load_w(w_hid_hbm, 0, "w_hid_raw", (half(0), half(1)))
+            y_raw[0, 0] = load_f32(y_hbm, 0, 0, "y_raw")
+            load_grad(0, 0)
+            w_hid_raw[1] = load_w(w_hid_hbm, 1, "w_hid_raw")
+            y_raw[1, 0] = load_f32(y_hbm, 1, 0, "y_raw")
+            load_grad(1, 0)
+            mem_raw[0, 0] = load_f32(mem_hbm, 0, 0, "mem_raw")
+            mem_raw[1, 0] = load_f32(mem_hbm, 1, 0, "mem_raw")
+            y_raw[0, 1] = load_f32(y_hbm, 0, 1, "y_raw")
+            load_grad(0, 1)
+
+            for c in range(2):
+                interleave_w(w_hid_raw[0], ("h", 0), c, True, "VS"[c])
+            square_y(0, 0)
+            for c in range(2):
+                quantize(w_hid_q, E4M3, 0, half(c), w_grouped[("h", 0), c])
+            make_dz2(0, 0)
+            interleave_w(w_hid_raw[1], ("h", 1), 1, True, "S")
+            interleave_w(w_hid_raw[1], ("h", 1), 0, True, "V")
+            square_y(1, 0)
+            quantize_dz2(0, 0)
+            for c in range(2):
+                quantize(w_hid_q, E4M3, 1, half(c), w_grouped[("h", 1), c])
+            make_dz2(1, 0)
+            quantize_dz2(1, 0)
+            y_raw[1, 1] = load_f32(y_hbm, 1, 1, "y_raw")
+            load_grad(1, 1)
+            mem_raw[0, 1] = load_f32(mem_hbm, 0, 1, "mem_raw")
+
+            dz1_t_grouped, x_t_grouped = {}, {}
+            for g in range(2):
+                square_mem(g, 0)
+                make_dz1(g, 0, hidden_products(g, 0))
+            mem_raw[1, 1] = load_f32(mem_hbm, 1, 1, "mem_raw")
+            load_x(0)
+            load_x(1)
+            w_rg_raw[0] = load_w(w_rg_hbm, 0, "w_rg_raw")
+            w_rg_raw[1] = load_w(w_rg_hbm, 1, "w_rg_raw")
+            square_y(0, 1)
+            dz1_t_grouped[0] = transposed_group(dz1[0], 0, "SS")
+            dz1_t_grouped[1] = transposed_group(dz1[1], 0, "SS")
+            square_y(1, 1)
+            make_dz2(0, 1)
+            for g in range(2):
+                quantize(dz1_t_q, E5M2, 0, half(g), dz1_t_grouped[g])
+            quantize_dz2(0, 1)
+            make_dz2(1, 1)
+            quantize_dz2(1, 1)
+            square_mem(0, 1)
+            square_mem(1, 1)
+            make_dz1(0, 1, hidden_products(0, 1))
+            dz1_t_grouped[0] = transposed_group(dz1[0], 1, "SS")
+            make_dz1(1, 1, hidden_products(1, 1))
+            for h in range(2):
+                x_t_grouped[h] = transposed_group(x_raw[0], h, "SS")
+            dz1_grouped = {}
+            dz1_grouped[0] = interleave_dz1(0, 0, "V")
+            quantize(dz1_t_q, E5M2, 1, half(0), dz1_t_grouped[0])
+            for h in range(2):
+                quantize(x_t_q, E4M3, h, half(0), x_t_grouped[h])
+            dz1_t_grouped[1] = transposed_group(dz1[1], 1, "VV")
+            quantize(dz1_q, E5M2, 0, half(0), dz1_grouped[0])
+            quantize(dz1_t_q, E5M2, 1, half(1), dz1_t_grouped[1])
+            for z in range(2):
+                out_1_tiles(0, z, 0, "SS")
+            for h in range(2):
+                x_t_grouped[h] = transposed_group(x_raw[1], h, "SV")
+            dz1_grouped[1] = interleave_dz1(1, 0, "V")
+            for h in range(2):
+                quantize(x_t_q, E4M3, h, half(1), x_t_grouped[h])
+            quantize(dz1_q, E5M2, 1, half(0), dz1_grouped[1])
+            for z in range(2):
+                out_1_tiles(1, z, 0, "SS")
+            for k in range(2):
+                for c in range(2):
+                    interleave_w(w_rg_raw[k], ("r", k), c, False, "VS"[c & k])
+                for g in range(1):
+                    out_1_tiles(k, 0, 1, "SS")
+                for c in range(2):
+                    quantize(w_rg_q, E4M3, k, half(c), w_grouped[("r", k), c])
+            for g in range(2):
+                out_1_tiles(g, 1, 1, "SS")
+            dz1_grouped = [interleave_dz1(g, 1, "V") for g in range(2)]
+            for g in range(2):
+                quantize(dz1_q, E5M2, g, half(1), dz1_grouped[g])
+            for h in range(2):
+                for z in range(4):
+                    out_0_tiles(h, z, "SV" if h else "SS")

@@ -81,26 +81,29 @@ def tile_pt_grumb_pb_v_kernel(
                 in_=grouped[:].rearrange("p n j -> p (n j)"),
             )
 
+        def product_pass(k, out, lhs, lhs_dtype, lhs_cols, rhs, rhs_dtype, rhs_cols):
+            nc.tensor.matmul_mx(
+                out=out,
+                lhsT=lhs[0][:, k, lhs_cols].bitcast(lhs_dtype),
+                lhsT_scale=lhs[1][:, k, lhs_cols],
+                rhs=rhs[0][:, k, rhs_cols].bitcast(rhs_dtype),
+                rhs_scale=rhs[1][:, k, rhs_cols],
+                start=(k == 0),
+                stop=(k == 1),
+            )
+
         def product(out, lhs, lhs_dtype, lhs_cols, rhs, rhs_dtype, rhs_cols):
             for k in range(2):
-                nc.tensor.matmul_mx(
-                    out=out,
-                    lhsT=lhs[0][:, k, lhs_cols].bitcast(lhs_dtype),
-                    lhsT_scale=lhs[1][:, k, lhs_cols],
-                    rhs=rhs[0][:, k, rhs_cols].bitcast(rhs_dtype),
-                    rhs_scale=rhs[1][:, k, rhs_cols],
-                    start=(k == 0),
-                    stop=(k == 1),
-                )
+                product_pass(k, out, lhs, lhs_dtype, lhs_cols, rhs, rhs_dtype, rhs_cols)
 
         def load_w(hbm, k, name, pieces=(slice(0, SIZE),)):
-            t = raw.tile([P, PACK, SIZE], BF16, name=name, tag="w_raw", align_bytes=64, bufs=3)
+            t = raw.tile([P, PACK, SIZE], BF16, name=name, tag="w_raw", align_bytes=64, bufs=4)
             for cols in pieces:
                 nc.sync.dma_start(out=t[:, :, cols], in_=hbm[k][:, :, cols])
             return t
 
         def load_f32(hbm, k, h, name):
-            t = raw.tile([P, PACK, HALF], F32, name=name, tag="f32_raw", align_bytes=64, bufs=5)
+            t = raw.tile([P, PACK, HALF], F32, name=name, tag="f32_raw", align_bytes=64, bufs=4)
             nc.sync.dma_start(out=t[:], in_=hbm[k][:, :, half(h)])
             return t
 
@@ -163,22 +166,22 @@ def tile_pt_grumb_pb_v_kernel(
                 )
             w_grouped[key, c] = grouped
 
-        def hidden_products(g, h):
-            dh = []
-            for t in range(PACK):
-                ps = bank([P, HALF], F32)
-                first = g * HALF + t * P
-                product(ps[:], w_hid_q, E4M3, slice(first, first + P), dz2_q, E5M2, half(h))
-                dh.append(ps)
-            return dh
+        dh = {}
 
-        def make_dz1(g, h, dh):
+        def hidden_pass(k, g, h):
+            for t in range(PACK):
+                if k == 0:
+                    dh[g, h, t] = bank([P, HALF], F32)
+                first = g * HALF + t * P
+                product_pass(k, dh[g, h, t][:], w_hid_q, E4M3, slice(first, first + P), dz2_q, E5M2, half(h))
+
+        def make_dz1(g, h):
             for t in range(PACK):
                 nc.vector.scalar_tensor_tensor(
                     out=dz1[g][:, t, half(h)],
                     in0=mem_raw[g, h][:, t, :],
                     scalar=0.25,
-                    in1=dh[t][:],
+                    in1=dh[g, h, t][:],
                     op0=ALU.subtract,
                     op1=ALU.mult,
                 )
@@ -238,9 +241,9 @@ def tile_pt_grumb_pb_v_kernel(
             y_raw[1, 0] = load_f32(y_hbm, 1, 0, "y_raw")
             load_grad(1, 0)
             mem_raw[0, 0] = load_f32(mem_hbm, 0, 0, "mem_raw")
+            w_rg_raw[0] = load_w(w_rg_hbm, 0, "w_rg_raw")
             mem_raw[1, 0] = load_f32(mem_hbm, 1, 0, "mem_raw")
-            y_raw[0, 1] = load_f32(y_hbm, 0, 1, "y_raw")
-            load_grad(0, 1)
+            w_rg_raw[1] = load_w(w_rg_hbm, 1, "w_rg_raw")
 
             for c in range(2):
                 interleave_w(w_hid_raw[0], ("h", 0), c, True, "VS"[c])
@@ -248,74 +251,87 @@ def tile_pt_grumb_pb_v_kernel(
             for c in range(2):
                 quantize(w_hid_q, E4M3, 0, half(c), w_grouped[("h", 0), c])
             make_dz2(0, 0)
+            y_raw[0, 1] = load_f32(y_hbm, 0, 1, "y_raw")
+            load_grad(0, 1)
             interleave_w(w_hid_raw[1], ("h", 1), 1, True, "S")
             interleave_w(w_hid_raw[1], ("h", 1), 0, True, "V")
-            square_y(1, 0)
             quantize_dz2(0, 0)
+            for g in range(2):
+                hidden_pass(0, g, 0)
+            square_y(1, 0)
             for c in range(2):
                 quantize(w_hid_q, E4M3, 1, half(c), w_grouped[("h", 1), c])
             make_dz2(1, 0)
-            quantize_dz2(1, 0)
             y_raw[1, 1] = load_f32(y_hbm, 1, 1, "y_raw")
             load_grad(1, 1)
-            mem_raw[0, 1] = load_f32(mem_hbm, 0, 1, "mem_raw")
-
-            dz1_t_grouped, x_t_grouped = {}, {}
+            square_mem(0, 0)
+            quantize_dz2(1, 0)
             for g in range(2):
-                square_mem(g, 0)
-                make_dz1(g, 0, hidden_products(g, 0))
+                hidden_pass(1, g, 0)
+
+            dz1_t_grouped, x_t_grouped, dz1_grouped = {}, {}, {}
+            make_dz1(0, 0)
+            mem_raw[0, 1] = load_f32(mem_hbm, 0, 1, "mem_raw")
+            interleave_w(w_rg_raw[0], ("r", 0), 0, False, "S")
+            interleave_w(w_rg_raw[0], ("r", 0), 1, False, "V")
+            square_mem(1, 0)
+            quantize(w_rg_q, E4M3, 0, half(0), w_grouped[("r", 0), 0])
+            quantize(w_rg_q, E4M3, 0, half(1), w_grouped[("r", 0), 1])
+            make_dz1(1, 0)
             mem_raw[1, 1] = load_f32(mem_hbm, 1, 1, "mem_raw")
             load_x(0)
             load_x(1)
-            w_rg_raw[0] = load_w(w_rg_hbm, 0, "w_rg_raw")
-            w_rg_raw[1] = load_w(w_rg_hbm, 1, "w_rg_raw")
+            interleave_w(w_rg_raw[1], ("r", 1), 0, False, "S")
+            dz1_grouped[0] = interleave_dz1(0, 0, "V")
+            interleave_w(w_rg_raw[1], ("r", 1), 1, False, "V")
             square_y(0, 1)
+            dz1_grouped[1] = interleave_dz1(1, 0, "V")
+            quantize(w_rg_q, E4M3, 1, half(0), w_grouped[("r", 1), 0])
+            quantize(dz1_q, E5M2, 0, half(0), dz1_grouped[0])
+            quantize(w_rg_q, E4M3, 1, half(1), w_grouped[("r", 1), 1])
+            quantize(dz1_q, E5M2, 1, half(0), dz1_grouped[1])
+            make_dz2(0, 1)
+            square_y(1, 1)
             dz1_t_grouped[0] = transposed_group(dz1[0], 0, "SS")
             dz1_t_grouped[1] = transposed_group(dz1[1], 0, "SS")
-            square_y(1, 1)
-            make_dz2(0, 1)
+            quantize_dz2(0, 1)
+            for z in range(3):
+                out_0_tiles(0, z, "SS")
+            make_dz2(1, 1)
+            square_mem(0, 1)
+            for g in range(2):
+                hidden_pass(0, g, 1)
+            quantize_dz2(1, 1)
+            square_mem(1, 1)
             for g in range(2):
                 quantize(dz1_t_q, E5M2, 0, half(g), dz1_t_grouped[g])
-            quantize_dz2(0, 1)
-            make_dz2(1, 1)
-            quantize_dz2(1, 1)
-            square_mem(0, 1)
-            square_mem(1, 1)
-            make_dz1(0, 1, hidden_products(0, 1))
-            dz1_t_grouped[0] = transposed_group(dz1[0], 1, "SS")
-            make_dz1(1, 1, hidden_products(1, 1))
+            for g in range(2):
+                hidden_pass(1, g, 1)
+            make_dz1(0, 1)
+            out_0_tiles(0, 3, "SS")
+            make_dz1(1, 1)
             for h in range(2):
                 x_t_grouped[h] = transposed_group(x_raw[0], h, "SS")
-            dz1_grouped = {}
-            dz1_grouped[0] = interleave_dz1(0, 0, "V")
-            quantize(dz1_t_q, E5M2, 1, half(0), dz1_t_grouped[0])
+            dz1_t_grouped[0] = transposed_group(dz1[0], 1, "VV")
             for h in range(2):
                 quantize(x_t_q, E4M3, h, half(0), x_t_grouped[h])
+            quantize(dz1_t_q, E5M2, 1, half(0), dz1_t_grouped[0])
             dz1_t_grouped[1] = transposed_group(dz1[1], 1, "VV")
-            quantize(dz1_q, E5M2, 0, half(0), dz1_grouped[0])
-            quantize(dz1_t_q, E5M2, 1, half(1), dz1_t_grouped[1])
             for z in range(2):
                 out_1_tiles(0, z, 0, "SS")
+            dz1_grouped[0] = interleave_dz1(0, 1, "V")
+            quantize(dz1_t_q, E5M2, 1, half(1), dz1_t_grouped[1])
             for h in range(2):
                 x_t_grouped[h] = transposed_group(x_raw[1], h, "SV")
-            dz1_grouped[1] = interleave_dz1(1, 0, "V")
-            for h in range(2):
-                quantize(x_t_q, E4M3, h, half(1), x_t_grouped[h])
-            quantize(dz1_q, E5M2, 1, half(0), dz1_grouped[1])
+            quantize(dz1_q, E5M2, 0, half(1), dz1_grouped[0])
             for z in range(2):
                 out_1_tiles(1, z, 0, "SS")
-            for k in range(2):
-                for c in range(2):
-                    interleave_w(w_rg_raw[k], ("r", k), c, False, "VS"[c & k])
-                for g in range(1):
-                    out_1_tiles(k, 0, 1, "SS")
-                for c in range(2):
-                    quantize(w_rg_q, E4M3, k, half(c), w_grouped[("r", k), c])
-            for g in range(2):
-                out_1_tiles(g, 1, 1, "SS")
-            dz1_grouped = [interleave_dz1(g, 1, "V") for g in range(2)]
-            for g in range(2):
-                quantize(dz1_q, E5M2, g, half(1), dz1_grouped[g])
             for h in range(2):
-                for z in range(4):
-                    out_0_tiles(h, z, "SV" if h else "SS")
+                quantize(x_t_q, E4M3, h, half(1), x_t_grouped[h])
+            dz1_grouped[1] = interleave_dz1(1, 1, "V")
+            quantize(dz1_q, E5M2, 1, half(1), dz1_grouped[1])
+            for g in range(2):
+                for z in range(2):
+                    out_1_tiles(g, z, 1, "SV")
+            for z in range(4):
+                out_0_tiles(1, z, "SV")

@@ -20,6 +20,22 @@ HALF = 512
 FLOPS = 3 * 2 * SIZE * SIZE * SIZE
 BYTES = 4 * SIZE * SIZE * 2 + 2 * SIZE * SIZE * 4 + 2 * SIZE * SIZE * 4
 
+ORDER = """
+Lh0 Lh1 Ly00 Lg00 Ly10 Lg10 Lr0
+Ih00V Ih11S Ih01V Ih10V Qh00 Qh01 Qh10 Qh11
+Lr1 Lm00 Lm10 Lx0
+Sy00 Zz00 Qz00 Hp0000 Hp0001 Hp0002 Hp0003 Hp0100 Hp0101 Hp0102 Hp0103 Ly01 Lg01 Sy10 Zz10 Ir00S Ir01V Ir10V Qz10 Hp1000 Hp1001 Hp1002 Hp1003 Ir11S Qr00 Qr01 Qr10 Qr11
+Ly11 Lg11 Lx1 Sm00 Hp1100 Hp1101 Hp1102 Hp1103 Dz000 Dz001 Dz002 Dz003 Lm01 Sm10 Tt000 Xt000 Cc000S I100S Dz100 Dz101 Dz102 Dz103 Lm11 Tt001 Xt001 Tt100 Tt101
+Sy01 Xc000V Q100 I110V Cc001V Xc001S Q110 Cc101V Sy11 Cc100S
+P0000 P0001 P0010 P0011 E0000S E0010S Zz01 Zz11 Xt011 Xc011S P0020 P0021 E0001V W000 E0011S W001 E0020S Qz01 Qz11 E0021S W002 Sm01
+P0030 P0031 Xt110 Xt111 Xt010 E0030S Qt00 Qt01 Xc110S Xc111S Sm11 Xc010V E0031V W003
+Hp0010 Hp1010 Dz010 Hp0011 Hp1011 Dz011 Hp0012 Hp1012 Dz012 Hp0013 Hp1013 Dz013 Qx00 Qx10
+Hp0110 Hp1110 Xt100 Tt010 Tt011 Xt101 Cc010V Cc011S Dz110 Qt10 Xc100S Xc101S Qx01 Qx11 Hp0111 Hp0112 Hp0113 Hp1111 Hp1112 Hp1113 I101S Dz111 Dz112 Dz113
+P10000 P10001 P10100 P10101 E10000S E10001S W1000 E10100S E10101S W1010 I111V P10010 P10011 P10110 P10111 Q101 Q111 E10010S E10011S W1001 E10110S E10111V W1011
+Tt110 Tt111 Cc110S P0100 P0101 P0110 Cc111V E0100S E0101V W010 P0111 E0110S E0111V W011 P0120 P0121 Qt11 E0120S E0121V W012 P0130 P0131 E0130S E0131V W013
+P11000 P11001 E11000S E11001V W1100 P11100 P11101 E11100S E11101V W1110 P11010 P11011 E11010S E11011V W1101 P11110 P11111 E11110S E11111V W1111
+"""
+
 
 def tile_pt_grumb_pb_v_kernel(
     tc, x, out0, mem0, inp_out, w_readgate, w_rec_readgate, w_mem_readgate, w_hid_out, mem_out, y, grad_out, out_0, out_1
@@ -30,23 +46,21 @@ def tile_pt_grumb_pb_v_kernel(
     y_hbm = y.rearrange("(k p j) b -> k p j b", p=P, j=PACK)
     grad_hbm = grad_out.rearrange("(k p j) b -> k p j b", p=P, j=PACK)
     mem_hbm = mem_out.rearrange("(g p t) b -> g p t b", p=P, t=PACK)
-    x_hbm = x.rearrange("(n a p) b -> n p a b", p=P, a=4)
+    x_hbm = x.rearrange("(n a p) b -> n p a b", p=P, a=PACK)
     out_0_hbm = out_0.rearrange("(z a p) b -> z p a b", p=P, a=2)
     out_1_hbm = out_1.rearrange("(g p t) i -> g p t i", p=P, t=PACK)
 
     with ExitStack() as ctx:
         keep = ctx.enter_context(tc.tile_pool(name="keep", bufs=1))
         raw = ctx.enter_context(tc.tile_pool(name="raw", bufs=1))
-        work = ctx.enter_context(tc.tile_pool(name="work", bufs=6))
+        work = ctx.enter_context(tc.tile_pool(name="work", bufs=1))
         psum = ctx.enter_context(tc.psum_pool(name="psum", bufs=8))
 
         def keep_tile(shape, dtype, name):
             return keep.tile(shape, dtype, name=name, tag=name, align_bytes=64)
 
         def codes_pair(name):
-            codes = keep_tile([P, 2, SIZE], U32, name + "_codes")
-            scales = keep_tile([P, 2, SIZE], U8, name + "_scales")
-            return codes, scales
+            return keep_tile([P, 2, SIZE], U32, name + "_codes"), keep_tile([P, 2, SIZE], U8, name + "_scales")
 
         w_hid_q = codes_pair("w_hid")
         w_rg_q = codes_pair("w_rg")
@@ -55,14 +69,18 @@ def tile_pt_grumb_pb_v_kernel(
         dz1_t_q = codes_pair("dz1_t")
         x_t_q = codes_pair("x_t")
         dz1 = [keep_tile([P, PACK, SIZE], BF16, "dz1_%d" % g) for g in range(2)]
-        ident_f32 = keep_tile([P, P], F32, "ident_f32")
+        ident = keep_tile([P, P], F32, "ident")
         minus_half = keep_tile([P, 1], F32, "minus_half")
+        held = {}
 
-        def bank(shape, dtype):
-            return psum.tile(shape, dtype, name="bank", tag="bank")
+        def raw_tile(shape, dtype, tag, bufs):
+            return raw.tile(shape, dtype, name=tag, tag=tag, align_bytes=64, bufs=bufs)
 
         def grouped_tile():
-            return work.tile([P, HALF, PACK], BF16, name="grouped", tag="grouped", align_bytes=64, bufs=6)
+            return work.tile([P, HALF, PACK], BF16, name="grouped", tag="grouped", align_bytes=64, bufs=8)
+
+        def bank(shape):
+            return psum.tile(shape, F32, name="bank", tag="bank")
 
         def half(n):
             return slice(n * HALF, (n + 1) * HALF)
@@ -73,265 +91,201 @@ def tile_pt_grumb_pb_v_kernel(
             else:
                 nc.vector.tensor_copy(out=out, in_=in_)
 
-        def quantize(pair, dtype, row, cols, grouped):
+        def quantize(pair, dtype, row, col, grouped):
             codes, scales = pair
             nc.vector.quantize_mx(
-                out=codes[:, row, cols].bitcast(dtype),
-                scales=scales[:, row, cols],
+                out=codes[:, row, half(col)].bitcast(dtype),
+                scales=scales[:, row, half(col)],
                 in_=grouped[:].rearrange("p n j -> p (n j)"),
             )
 
-        def product_pass(k, out, lhs, lhs_dtype, lhs_cols, rhs, rhs_dtype, rhs_cols):
+        def product_pass(k, out, lhs, lhs_dtype, lhs_first, rhs, rhs_dtype, rhs_half):
+            lhs_cols = slice(lhs_first, lhs_first + P)
             nc.tensor.matmul_mx(
                 out=out,
                 lhsT=lhs[0][:, k, lhs_cols].bitcast(lhs_dtype),
                 lhsT_scale=lhs[1][:, k, lhs_cols],
-                rhs=rhs[0][:, k, rhs_cols].bitcast(rhs_dtype),
-                rhs_scale=rhs[1][:, k, rhs_cols],
+                rhs=rhs[0][:, k, half(rhs_half)].bitcast(rhs_dtype),
+                rhs_scale=rhs[1][:, k, half(rhs_half)],
                 start=(k == 0),
                 stop=(k == 1),
             )
 
-        def product(out, lhs, lhs_dtype, lhs_cols, rhs, rhs_dtype, rhs_cols):
-            for k in range(2):
-                product_pass(k, out, lhs, lhs_dtype, lhs_cols, rhs, rhs_dtype, rhs_cols)
-
-        def load_w(hbm, k, name, pieces=(slice(0, SIZE),)):
-            t = raw.tile([P, PACK, SIZE], BF16, name=name, tag="w_raw", align_bytes=64, bufs=4)
+        def load_weight(key, hbm, k, pieces):
+            held[key, k] = raw_tile([P, PACK, SIZE], BF16, "w_raw", 3)
             for cols in pieces:
-                nc.sync.dma_start(out=t[:, :, cols], in_=hbm[k][:, :, cols])
-            return t
+                nc.sync.dma_start(out=held[key, k][:, :, cols], in_=hbm[k][:, :, cols])
 
-        def load_f32(hbm, k, h, name):
-            t = raw.tile([P, PACK, HALF], F32, name=name, tag="f32_raw", align_bytes=64, bufs=4)
-            nc.sync.dma_start(out=t[:], in_=hbm[k][:, :, half(h)])
-            return t
+        def load_w_hid(k):
+            load_weight("w_hid_raw", w_hid_hbm, k, [half(0), half(1)] if k == 0 else [slice(0, SIZE)])
 
-        y_raw, mem_raw, w_hid_raw, w_rg_raw, grad_raw, x_raw = {}, {}, {}, {}, {}, {}
+        def load_w_rg(k):
+            load_weight("w_rg_raw", w_rg_hbm, k, [slice(0, SIZE)])
+
+        def load_part(key, hbm, dtype, tag, bufs, k, h):
+            held[key, k, h] = raw_tile([P, PACK, HALF], dtype, tag, bufs)
+            nc.sync.dma_start(out=held[key, k, h][:], in_=hbm[k][:, :, half(h)])
+
+        def load_y(k, h):
+            load_part("y_raw", y_hbm, F32, "f32_raw", 4, k, h)
+
+        def load_mem(g, h):
+            load_part("mem_raw", mem_hbm, F32, "f32_raw", 4, g, h)
 
         def load_grad(k, h):
-            t = raw.tile([P, PACK, HALF], BF16, name="grad_raw", tag="grad_raw", align_bytes=64, bufs=4)
-            nc.sync.dma_start(out=t[:], in_=grad_hbm[k][:, :, half(h)])
-            grad_raw[k, h] = t
+            load_part("grad_raw", grad_hbm, BF16, "grad_raw", 4, k, h)
 
         def load_x(n):
-            t = raw.tile([P, 4, SIZE], BF16, name="x_raw", tag="x_raw", align_bytes=64, bufs=2)
-            nc.sync.dma_start(out=t[:], in_=x_hbm[n])
-            x_raw[n] = t
-
-        y_squared = {}
+            held["x_raw", n] = raw_tile([P, PACK, SIZE], BF16, "x_raw", 2)
+            nc.sync.dma_start(out=held["x_raw", n][:], in_=x_hbm[n])
 
         def square_y(k, h):
             t = work.tile([P, HALF, PACK], F32, name="y_squared", tag="y_squared", align_bytes=64, bufs=2)
             nc.scalar.activation(
                 out=t[:].rearrange("p (c i) j -> p c j i", i=4),
-                in_=y_raw[k, h][:].rearrange("p j (c i) -> p c j i", i=4),
+                in_=held["y_raw", k, h][:].rearrange("p j (c i) -> p c j i", i=4),
                 func=ACT.Square,
             )
-            y_squared[k, h] = t
+            held["y_squared", k, h] = t
 
         def square_mem(g, h):
-            t = mem_raw[g, h]
+            t = held["mem_raw", g, h]
             nc.scalar.activation(out=t[:], in_=t[:], func=ACT.Square, bias=minus_half[:])
-
-        dz2_grouped = {}
 
         def make_dz2(k, h):
             grouped = grouped_tile()
             nc.vector.scalar_tensor_tensor(
                 out=grouped[:],
-                in0=y_squared[k, h][:],
+                in0=held["y_squared", k, h][:],
                 scalar=1.0,
-                in1=grad_raw[k, h][:].rearrange("p j b -> p b j"),
+                in1=held["grad_raw", k, h][:].rearrange("p j b -> p b j"),
                 op0=ALU.subtract,
                 op1=ALU.mult,
             )
-            dz2_grouped[k, h] = grouped
+            held["dz2", k, h] = grouped
 
-        def quantize_dz2(k, h):
-            quantize(dz2_q, E5M2, k, half(h), dz2_grouped[k, h])
-
-        w_grouped = {}
-
-        def interleave_w(raw_tile, key, c, permuted, engine):
-            cols = raw_tile[:, :, half(c)]
-            grouped = grouped_tile()
-            if permuted:
-                move(engine, grouped[:].rearrange("p (t m) j -> p t m j", t=PACK), cols.rearrange("p j (m t) -> p t m j", t=PACK))
-            else:
-                move(
-                    engine,
-                    grouped[:].rearrange("p (c i) j -> p c j i", i=4),
-                    cols.rearrange("p j (c i) -> p c j i", i=4),
-                )
-            w_grouped[key, c] = grouped
-
-        dh = {}
-
-        def hidden_pass(k, g, h):
-            for t in range(PACK):
-                if k == 0:
-                    dh[g, h, t] = bank([P, HALF], F32)
-                first = g * HALF + t * P
-                product_pass(k, dh[g, h, t][:], w_hid_q, E4M3, slice(first, first + P), dz2_q, E5M2, half(h))
-
-        def make_dz1(g, h):
-            for t in range(PACK):
-                nc.vector.scalar_tensor_tensor(
-                    out=dz1[g][:, t, half(h)],
-                    in0=mem_raw[g, h][:, t, :],
-                    scalar=0.25,
-                    in1=dh[g, h, t][:],
-                    op0=ALU.subtract,
-                    op1=ALU.mult,
-                )
-
-        def transposed_group(source, h, engines):
-            words = source[:].rearrange("p a b -> p (a b)").bitcast(F32)
-            grouped = grouped_tile()
-            target = grouped[:].rearrange("p n j -> p (n j)").bitcast(F32)
-            for z in range(2):
-                ps = bank([P, 2, 2, P], F32)
-                for a in range(2):
-                    for u in range(2):
-                        first = (2 * z + a) * HALF + h * 2 * P + u
-                        nc.tensor.transpose(ps[:, a, u, :], words[:, first : first + 2 * P - 1 : 2], ident_f32[:])
-                move(
-                    engines[z],
-                    target[:, z * HALF : (z + 1) * HALF].rearrange("p (a r u) -> p a r u", a=2, u=2),
-                    ps[:].rearrange("p a u r -> p a r u"),
-                )
-            return grouped
-
-        def interleave_dz1(g, h, engine):
+        def interleave_w_hid(k, c, engine):
             grouped = grouped_tile()
             move(
                 engine,
-                grouped[:].rearrange("p (c i) t -> p c t i", i=4),
-                dz1[g][:, :, half(h)].rearrange("p t (c i) -> p c t i", i=4),
+                grouped[:].rearrange("p (t m) j -> p t m j", t=PACK),
+                held["w_hid_raw", k][:, :, half(c)].rearrange("p j (m t) -> p t m j", t=PACK),
+            )
+            held["w_hid", k, c] = grouped
+
+        def interleave(engine, source):
+            grouped = grouped_tile()
+            move(
+                engine,
+                grouped[:].rearrange("p (c i) j -> p c j i", i=4),
+                source.rearrange("p j (c i) -> p c j i", i=4),
             )
             return grouped
 
-        def out_0_tiles(h, z, engines):
-            stage = work.tile([P, 2, HALF], F32, name="stage", tag="stage", align_bytes=64, bufs=5)
-            for a in range(2):
-                ps = bank([P, HALF], F32)
-                first = (2 * z + a) * P
-                product(ps[:], w_rg_q, E4M3, slice(first, first + P), dz1_q, E5M2, half(h))
-                move(engines[a], stage[:, a, :], ps[:])
-            nc.sync.dma_start(out=out_0_hbm[z][:, :, half(h)], in_=stage[:])
+        def interleave_w_rg(k, c, engine):
+            held["w_rg", k, c] = interleave(engine, held["w_rg_raw", k][:, :, half(c)])
 
-        def out_1_tiles(g, z, n, engines):
-            stage = work.tile([P, 2, HALF], F32, name="stage", tag="stage", align_bytes=64, bufs=5)
+        def interleave_dz1(g, h, engine):
+            held["dz1", g, h] = interleave(engine, dz1[g][:, :, half(h)])
+
+        def hidden_pass(k, g, h, t):
+            if k == 0:
+                held["dh", g, h, t] = bank([P, HALF])
+            product_pass(k, held["dh", g, h, t][:], w_hid_q, E4M3, g * HALF + t * P, dz2_q, E5M2, h)
+
+        def make_dz1(g, h, t):
+            nc.vector.scalar_tensor_tensor(
+                out=dz1[g][:, t, half(h)],
+                in0=held["mem_raw", g, h][:, t, :],
+                scalar=0.25,
+                in1=held["dh", g, h, t][:],
+                op0=ALU.subtract,
+                op1=ALU.mult,
+            )
+
+        def transpose(key, source, h, z):
+            words = source[:].rearrange("p a b -> p (a b)").bitcast(F32)
+            ps = bank([P, 2, 2, P])
             for a in range(2):
-                ps = bank([P, HALF], F32)
-                first = g * HALF + (2 * z + a) * P
-                product(ps[:], dz1_t_q, E5M2, slice(first, first + P), x_t_q, E4M3, half(n))
-                move(engines[a], stage[:, a, :], ps[:])
-            nc.sync.dma_start(out=out_1_hbm[g][:, 2 * z : 2 * z + 2, half(n)], in_=stage[:])
+                for u in range(2):
+                    first = (2 * z + a) * HALF + h * 2 * P + u
+                    nc.tensor.transpose(ps[:, a, u, :], words[:, first : first + 2 * P - 1 : 2], ident[:])
+            held[key, h, z] = ps
+
+        def copy_transposed(key, h, z, engine):
+            if (key, h) not in held:
+                held[key, h] = grouped_tile()
+            words = held[key, h][:].rearrange("p n j -> p (n j)").bitcast(F32)
+            move(
+                engine,
+                words[:, half(z)].rearrange("p (a r u) -> p a r u", a=2, u=2),
+                held[key, h, z][:].rearrange("p a u r -> p a r u"),
+            )
+
+        def stage_for(key):
+            if key not in held:
+                held[key] = work.tile([P, 2, HALF], F32, name="stage", tag="stage", align_bytes=64, bufs=5)
+            return held[key]
+
+        def out_0_product(h, z, a):
+            held["ps_0", h, z, a] = bank([P, HALF])
+            for k in range(2):
+                product_pass(k, held["ps_0", h, z, a][:], w_rg_q, E4M3, (2 * z + a) * P, dz1_q, E5M2, h)
+
+        def out_0_copy(h, z, a, engine):
+            move(engine, stage_for(("stage_0", h, z))[:, a, :], held["ps_0", h, z, a][:])
+
+        def out_0_store(h, z):
+            nc.sync.dma_start(out=out_0_hbm[z][:, :, half(h)], in_=held["stage_0", h, z][:])
+
+        def out_1_product(g, z, n, a):
+            held["ps_1", g, z, n, a] = bank([P, HALF])
+            for k in range(2):
+                product_pass(k, held["ps_1", g, z, n, a][:], dz1_t_q, E5M2, g * HALF + (2 * z + a) * P, x_t_q, E4M3, n)
+
+        def out_1_copy(g, z, n, a, engine):
+            move(engine, stage_for(("stage_1", g, z, n))[:, a, :], held["ps_1", g, z, n, a][:])
+
+        def out_1_store(g, z, n):
+            nc.sync.dma_start(out=out_1_hbm[g][:, 2 * z : 2 * z + 2, half(n)], in_=held["stage_1", g, z, n][:])
+
+        steps = {
+            "Lr": load_w_rg,
+            "Lh": load_w_hid,
+            "Ly": load_y,
+            "Lm": load_mem,
+            "Lg": load_grad,
+            "Lx": load_x,
+            "Sy": square_y,
+            "Sm": square_mem,
+            "Zz": make_dz2,
+            "Ih": interleave_w_hid,
+            "Ir": interleave_w_rg,
+            "I1": interleave_dz1,
+            "Hp": hidden_pass,
+            "Dz": make_dz1,
+            "Qh": lambda k, c: quantize(w_hid_q, E4M3, k, c, held["w_hid", k, c]),
+            "Qr": lambda k, c: quantize(w_rg_q, E4M3, k, c, held["w_rg", k, c]),
+            "Qz": lambda k, h: quantize(dz2_q, E5M2, k, h, held["dz2", k, h]),
+            "Q1": lambda g, h: quantize(dz1_q, E5M2, g, h, held["dz1", g, h]),
+            "Qt": lambda h, g: quantize(dz1_t_q, E5M2, h, g, held[("dz1_t", g), h]),
+            "Qx": lambda h, n: quantize(x_t_q, E4M3, h, n, held[("x_t", n), h]),
+            "Tt": lambda g, h, z: transpose(("dz1_t", g), dz1[g], h, z),
+            "Cc": lambda g, h, z, engine: copy_transposed(("dz1_t", g), h, z, engine),
+            "Xt": lambda n, h, z: transpose(("x_t", n), held["x_raw", n], h, z),
+            "Xc": lambda n, h, z, engine: copy_transposed(("x_t", n), h, z, engine),
+            "P0": out_0_product,
+            "E0": out_0_copy,
+            "W0": out_0_store,
+            "P1": out_1_product,
+            "E1": out_1_copy,
+            "W1": out_1_store,
+        }
 
         nc.vector.memset(minus_half[:], -0.5)
-        make_identity(nc, ident_f32[:])
+        make_identity(nc, ident[:])
 
         with tc.manual_schedule():
-            w_hid_raw[0] = load_w(w_hid_hbm, 0, "w_hid_raw", (half(0), half(1)))
-            y_raw[0, 0] = load_f32(y_hbm, 0, 0, "y_raw")
-            load_grad(0, 0)
-            w_hid_raw[1] = load_w(w_hid_hbm, 1, "w_hid_raw")
-            y_raw[1, 0] = load_f32(y_hbm, 1, 0, "y_raw")
-            load_grad(1, 0)
-            mem_raw[0, 0] = load_f32(mem_hbm, 0, 0, "mem_raw")
-            w_rg_raw[0] = load_w(w_rg_hbm, 0, "w_rg_raw")
-            mem_raw[1, 0] = load_f32(mem_hbm, 1, 0, "mem_raw")
-            w_rg_raw[1] = load_w(w_rg_hbm, 1, "w_rg_raw")
-
-            for c in range(2):
-                interleave_w(w_hid_raw[0], ("h", 0), c, True, "VS"[c])
-            square_y(0, 0)
-            for c in range(2):
-                quantize(w_hid_q, E4M3, 0, half(c), w_grouped[("h", 0), c])
-            make_dz2(0, 0)
-            y_raw[0, 1] = load_f32(y_hbm, 0, 1, "y_raw")
-            load_grad(0, 1)
-            interleave_w(w_hid_raw[1], ("h", 1), 1, True, "S")
-            interleave_w(w_hid_raw[1], ("h", 1), 0, True, "V")
-            quantize_dz2(0, 0)
-            for g in range(2):
-                hidden_pass(0, g, 0)
-            square_y(1, 0)
-            for c in range(2):
-                quantize(w_hid_q, E4M3, 1, half(c), w_grouped[("h", 1), c])
-            make_dz2(1, 0)
-            y_raw[1, 1] = load_f32(y_hbm, 1, 1, "y_raw")
-            load_grad(1, 1)
-            square_mem(0, 0)
-            quantize_dz2(1, 0)
-            for g in range(2):
-                hidden_pass(1, g, 0)
-
-            dz1_t_grouped, x_t_grouped, dz1_grouped = {}, {}, {}
-            make_dz1(0, 0)
-            mem_raw[0, 1] = load_f32(mem_hbm, 0, 1, "mem_raw")
-            interleave_w(w_rg_raw[0], ("r", 0), 0, False, "S")
-            interleave_w(w_rg_raw[0], ("r", 0), 1, False, "V")
-            square_mem(1, 0)
-            quantize(w_rg_q, E4M3, 0, half(0), w_grouped[("r", 0), 0])
-            quantize(w_rg_q, E4M3, 0, half(1), w_grouped[("r", 0), 1])
-            make_dz1(1, 0)
-            mem_raw[1, 1] = load_f32(mem_hbm, 1, 1, "mem_raw")
-            load_x(0)
-            load_x(1)
-            interleave_w(w_rg_raw[1], ("r", 1), 0, False, "S")
-            dz1_grouped[0] = interleave_dz1(0, 0, "V")
-            interleave_w(w_rg_raw[1], ("r", 1), 1, False, "V")
-            square_y(0, 1)
-            dz1_grouped[1] = interleave_dz1(1, 0, "V")
-            quantize(w_rg_q, E4M3, 1, half(0), w_grouped[("r", 1), 0])
-            quantize(dz1_q, E5M2, 0, half(0), dz1_grouped[0])
-            quantize(w_rg_q, E4M3, 1, half(1), w_grouped[("r", 1), 1])
-            quantize(dz1_q, E5M2, 1, half(0), dz1_grouped[1])
-            make_dz2(0, 1)
-            square_y(1, 1)
-            dz1_t_grouped[0] = transposed_group(dz1[0], 0, "SS")
-            dz1_t_grouped[1] = transposed_group(dz1[1], 0, "SS")
-            quantize_dz2(0, 1)
-            for z in range(3):
-                out_0_tiles(0, z, "SS")
-            make_dz2(1, 1)
-            square_mem(0, 1)
-            for g in range(2):
-                hidden_pass(0, g, 1)
-            quantize_dz2(1, 1)
-            square_mem(1, 1)
-            for g in range(2):
-                quantize(dz1_t_q, E5M2, 0, half(g), dz1_t_grouped[g])
-            for g in range(2):
-                hidden_pass(1, g, 1)
-            make_dz1(0, 1)
-            out_0_tiles(0, 3, "SS")
-            make_dz1(1, 1)
-            for h in range(2):
-                x_t_grouped[h] = transposed_group(x_raw[0], h, "SS")
-            dz1_t_grouped[0] = transposed_group(dz1[0], 1, "VV")
-            for h in range(2):
-                quantize(x_t_q, E4M3, h, half(0), x_t_grouped[h])
-            quantize(dz1_t_q, E5M2, 1, half(0), dz1_t_grouped[0])
-            dz1_t_grouped[1] = transposed_group(dz1[1], 1, "VV")
-            for z in range(2):
-                out_1_tiles(0, z, 0, "SS")
-            dz1_grouped[0] = interleave_dz1(0, 1, "V")
-            quantize(dz1_t_q, E5M2, 1, half(1), dz1_t_grouped[1])
-            for h in range(2):
-                x_t_grouped[h] = transposed_group(x_raw[1], h, "SV")
-            quantize(dz1_q, E5M2, 0, half(1), dz1_grouped[0])
-            for z in range(2):
-                out_1_tiles(1, z, 0, "SS")
-            for h in range(2):
-                quantize(x_t_q, E4M3, h, half(1), x_t_grouped[h])
-            dz1_grouped[1] = interleave_dz1(1, 1, "V")
-            quantize(dz1_q, E5M2, 1, half(1), dz1_grouped[1])
-            for g in range(2):
-                for z in range(2):
-                    out_1_tiles(g, z, 1, "SV")
-            for z in range(4):
-                out_0_tiles(1, z, "SV")
+            for step in ORDER.split():
+                arguments = [int(c) if c in "0123" else c for c in step[2:]]
+                steps[step[:2]](*arguments)

from contextlib import ExitStack

import concourse.mybir as mybir
from concourse.masks import make_identity

F32 = mybir.dt.float32
BF16 = mybir.dt.bfloat16
U32 = mybir.dt.uint32
U8 = mybir.dt.uint8
E4M3 = mybir.dt.float8_e4m3fn_x4
E5M2 = mybir.dt.float8_e5m2_x4
ACT = mybir.ActivationFunctionType
ALU = mybir.AluOpType

SIZE = 1024
P = 128
PACK = 4
HALF = 512

FLOPS = 3 * 2 * SIZE * SIZE * SIZE
BYTES = 4 * SIZE * SIZE * 2 + 2 * SIZE * SIZE * 4 + 2 * SIZE * SIZE * 4

ORDER = """
Lh0 Lh1 Ly00 Lg00 Ly10 Lg10 Lr0
Ih00V Ih11S Ih01V Ih10V Qh00 Qh01 Qh10 Qh11
Lr1 Lm00 Lm10 Lx0
Sy00 Zz00 Qz00 Hp0000 Hp0001 Hp0002 Hp0003 Hp0100 Hp0101 Hp0102 Hp0103 Ly01 Lg01 Sy10 Zz10 Ir00S Ir01V Ir10V Qz10 Hp1000 Hp1001 Hp1002 Hp1003 Ir11S Qr00 Qr01 Qr10 Qr11
Ly11 Lg11 Lx1 Sm00 Hp1100 Hp1101 Hp1102 Hp1103 Dz000 Dz001 Dz002 Dz003 Lm01 Sm10 Tt000 Xt000 Cc000S I100S Dz100 Dz101 Dz102 Dz103 Lm11 Tt001 Xt001 Tt100 Tt101
Sy01 Xc000V Q100 I110V Cc001V Xc001S Q110 Cc101V Sy11 Cc100S
P0000 P0001 P0010 P0011 E0000S E0010S Zz01 Zz11 Xt011 Xc011S P0020 P0021 E0001V W000 E0011S W001 E0020S Qz01 Qz11 E0021S W002 Sm01
P0030 P0031 Xt110 Xt111 Xt010 E0030S Qt00 Qt01 Xc110S Xc111S Sm11 Xc010V E0031V W003
Hp0010 Hp1010 Dz010 Hp0011 Hp1011 Dz011 Hp0012 Hp1012 Dz012 Hp0013 Hp1013 Dz013 Qx00 Qx10
Hp0110 Hp1110 Xt100 Tt010 Tt011 Xt101 Cc010V Cc011S Dz110 Qt10 Xc100S Xc101S Qx01 Qx11 Hp0111 Hp0112 Hp0113 Hp1111 Hp1112 Hp1113 I101S Dz111 Dz112 Dz113
P10000 P10001 P10100 P10101 E10000S E10001S W1000 E10100S E10101S W1010 I111V P10010 P10011 P10110 P10111 Q101 Q111 E10010S E10011S W1001 E10110S E10111V W1011
Tt110 Tt111 Cc110S P0100 P0101 P0110 Cc111V E0100S E0101V W010 P0111 E0110S E0111V W011 P0120 P0121 Qt11 E0120S E0121V W012 P0130 P0131 E0130S E0131V W013
P11000 P11001 E11000S E11001V W1100 P11100 P11101 E11100S E11101V W1110 P11010 P11011 E11010S E11011V W1101 P11110 P11111 E11110S E11111V W1111
"""


def tile_pt_grumb_pb_v_kernel(
    tc, x, out0, mem0, inp_out, w_readgate, w_rec_readgate, w_mem_readgate, w_hid_out, mem_out, y, grad_out, out_0, out_1
):
    nc = tc.nc
    w_hid_hbm = w_hid_out.rearrange("(k p j) m -> k p j m", p=P, j=PACK)
    w_rg_hbm = w_readgate.rearrange("(k p j) i -> k p j i", p=P, j=PACK)
    y_hbm = y.rearrange("(k p j) b -> k p j b", p=P, j=PACK)
    grad_hbm = grad_out.rearrange("(k p j) b -> k p j b", p=P, j=PACK)
    mem_hbm = mem_out.rearrange("(g p t) b -> g p t b", p=P, t=PACK)
    x_hbm = x.rearrange("(n a p) b -> n p a b", p=P, a=PACK)
    out_0_hbm = out_0.rearrange("(z a p) b -> z p a b", p=P, a=2)
    out_1_hbm = out_1.rearrange("(g p t) i -> g p t i", p=P, t=PACK)

    with ExitStack() as ctx:
        keep = ctx.enter_context(tc.tile_pool(name="keep", bufs=1))
        raw = ctx.enter_context(tc.tile_pool(name="raw", bufs=1))
        work = ctx.enter_context(tc.tile_pool(name="work", bufs=1))
        psum = ctx.enter_context(tc.psum_pool(name="psum", bufs=8))

        def keep_tile(shape, dtype, name):
            return keep.tile(shape, dtype, name=name, tag=name, align_bytes=64)

        def codes_pair(name):
            return keep_tile([P, 2, SIZE], U32, name + "_codes"), keep_tile([P, 2, SIZE], U8, name + "_scales")

        w_hid_q = codes_pair("w_hid")
        w_rg_q = codes_pair("w_rg")
        dz2_q = codes_pair("dz2")
        dz1_q = codes_pair("dz1")
        dz1_t_q = codes_pair("dz1_t")
        x_t_q = codes_pair("x_t")
        dz1 = [keep_tile([P, PACK, SIZE], BF16, "dz1_%d" % g) for g in range(2)]
        ident = keep_tile([P, P], F32, "ident")
        minus_half = keep_tile([P, 1], F32, "minus_half")
        held = {}

        def raw_tile(shape, dtype, tag, bufs):
            return raw.tile(shape, dtype, name=tag, tag=tag, align_bytes=64, bufs=bufs)

        def grouped_tile():
            return work.tile([P, HALF, PACK], BF16, name="grouped", tag="grouped", align_bytes=64, bufs=8)

        def bank(shape):
            return psum.tile(shape, F32, name="bank", tag="bank")

        def half(n):
            return slice(n * HALF, (n + 1) * HALF)

        def move(engine, out, in_):
            if engine == "S":
                nc.scalar.copy(out=out, in_=in_)
            else:
                nc.vector.tensor_copy(out=out, in_=in_)

        def quantize(pair, dtype, row, col, grouped):
            codes, scales = pair
            nc.vector.quantize_mx(
                out=codes[:, row, half(col)].bitcast(dtype),
                scales=scales[:, row, half(col)],
                in_=grouped[:].rearrange("p n j -> p (n j)"),
            )

        def product_pass(k, out, lhs, lhs_dtype, lhs_first, rhs, rhs_dtype, rhs_half):
            lhs_cols = slice(lhs_first, lhs_first + P)
            nc.tensor.matmul_mx(
                out=out,
                lhsT=lhs[0][:, k, lhs_cols].bitcast(lhs_dtype),
                lhsT_scale=lhs[1][:, k, lhs_cols],
                rhs=rhs[0][:, k, half(rhs_half)].bitcast(rhs_dtype),
                rhs_scale=rhs[1][:, k, half(rhs_half)],
                start=(k == 0),
                stop=(k == 1),
            )

        def load_weight(key, hbm, k, pieces):
            held[key, k] = raw_tile([P, PACK, SIZE], BF16, "w_raw", 3)
            for cols in pieces:
                nc.sync.dma_start(out=held[key, k][:, :, cols], in_=hbm[k][:, :, cols])

        def load_w_hid(k):
            load_weight("w_hid_raw", w_hid_hbm, k, [half(0), half(1)] if k == 0 else [slice(0, SIZE)])

        def load_w_rg(k):
            load_weight("w_rg_raw", w_rg_hbm, k, [slice(0, SIZE)])

        def load_part(key, hbm, dtype, tag, bufs, k, h):
            held[key, k, h] = raw_tile([P, PACK, HALF], dtype, tag, bufs)
            nc.sync.dma_start(out=held[key, k, h][:], in_=hbm[k][:, :, half(h)])

        def load_y(k, h):
            load_part("y_raw", y_hbm, F32, "f32_raw", 4, k, h)

        def load_mem(g, h):
            load_part("mem_raw", mem_hbm, F32, "f32_raw", 4, g, h)

        def load_grad(k, h):
            load_part("grad_raw", grad_hbm, BF16, "grad_raw", 4, k, h)

        def load_x(n):
            held["x_raw", n] = raw_tile([P, PACK, SIZE], BF16, "x_raw", 2)
            nc.sync.dma_start(out=held["x_raw", n][:], in_=x_hbm[n])

        def square_y(k, h):
            t = work.tile([P, HALF, PACK], F32, name="y_squared", tag="y_squared", align_bytes=64, bufs=2)
            nc.scalar.activation(
                out=t[:].rearrange("p (c i) j -> p c j i", i=4),
                in_=held["y_raw", k, h][:].rearrange("p j (c i) -> p c j i", i=4),
                func=ACT.Square,
            )
            held["y_squared", k, h] = t

        def square_mem(g, h):
            t = held["mem_raw", g, h]
            nc.scalar.activation(out=t[:], in_=t[:], func=ACT.Square, bias=minus_half[:])

        def make_dz2(k, h):
            grouped = grouped_tile()
            nc.vector.scalar_tensor_tensor(
                out=grouped[:],
                in0=held["y_squared", k, h][:],
                scalar=1.0,
                in1=held["grad_raw", k, h][:].rearrange("p j b -> p b j"),
                op0=ALU.subtract,
                op1=ALU.mult,
            )
            held["dz2", k, h] = grouped

        def interleave_w_hid(k, c, engine):
            grouped = grouped_tile()
            move(
                engine,
                grouped[:].rearrange("p (t m) j -> p t m j", t=PACK),
                held["w_hid_raw", k][:, :, half(c)].rearrange("p j (m t) -> p t m j", t=PACK),
            )
            held["w_hid", k, c] = grouped

        def interleave(engine, source):
            grouped = grouped_tile()
            move(
                engine,
                grouped[:].rearrange("p (c i) j -> p c j i", i=4),
                source.rearrange("p j (c i) -> p c j i", i=4),
            )
            return grouped

        def interleave_w_rg(k, c, engine):
            held["w_rg", k, c] = interleave(engine, held["w_rg_raw", k][:, :, half(c)])

        def interleave_dz1(g, h, engine):
            held["dz1", g, h] = interleave(engine, dz1[g][:, :, half(h)])

        def hidden_pass(k, g, h, t):
            if k == 0:
                held["dh", g, h, t] = bank([P, HALF])
            product_pass(k, held["dh", g, h, t][:], w_hid_q, E4M3, g * HALF + t * P, dz2_q, E5M2, h)

        def make_dz1(g, h, t):
            nc.vector.scalar_tensor_tensor(
                out=dz1[g][:, t, half(h)],
                in0=held["mem_raw", g, h][:, t, :],
                scalar=0.25,
                in1=held["dh", g, h, t][:],
                op0=ALU.subtract,
                op1=ALU.mult,
            )

        def transpose(key, source, h, z):
            words = source[:].rearrange("p a b -> p (a b)").bitcast(F32)
            ps = bank([P, 2, 2, P])
            for a in range(2):
                for u in range(2):
                    first = (2 * z + a) * HALF + h * 2 * P + u
                    nc.tensor.transpose(ps[:, a, u, :], words[:, first : first + 2 * P - 1 : 2], ident[:])
            held[key, h, z] = ps

        def copy_transposed(key, h, z, engine):
            if (key, h) not in held:
                held[key, h] = grouped_tile()
            words = held[key, h][:].rearrange("p n j -> p (n j)").bitcast(F32)
            move(
                engine,
                words[:, half(z)].rearrange("p (a r u) -> p a r u", a=2, u=2),
                held[key, h, z][:].rearrange("p a u r -> p a r u"),
            )

        def stage_for(key):
            if key not in held:
                held[key] = work.tile([P, 2, HALF], F32, name="stage", tag="stage", align_bytes=64, bufs=5)
            return held[key]

        def out_0_product(h, z, a):
            held["ps_0", h, z, a] = bank([P, HALF])
            for k in range(2):
                product_pass(k, held["ps_0", h, z, a][:], w_rg_q, E4M3, (2 * z + a) * P, dz1_q, E5M2, h)

        def out_0_copy(h, z, a, engine):
            move(engine, stage_for(("stage_0", h, z))[:, a, :], held["ps_0", h, z, a][:])

        def out_0_store(h, z):
            nc.sync.dma_start(out=out_0_hbm[z][:, :, half(h)], in_=held["stage_0", h, z][:])

        def out_1_product(g, z, n, a):
            held["ps_1", g, z, n, a] = bank([P, HALF])
            for k in range(2):
                product_pass(k, held["ps_1", g, z, n, a][:], dz1_t_q, E5M2, g * HALF + (2 * z + a) * P, x_t_q, E4M3, n)

        def out_1_copy(g, z, n, a, engine):
            move(engine, stage_for(("stage_1", g, z, n))[:, a, :], held["ps_1", g, z, n, a][:])

        def out_1_store(g, z, n):
            nc.sync.dma_start(out=out_1_hbm[g][:, 2 * z : 2 * z + 2, half(n)], in_=held["stage_1", g, z, n][:])

        steps = {
            "Lr": load_w_rg,
            "Lh": load_w_hid,
            "Ly": load_y,
            "Lm": load_mem,
            "Lg": load_grad,
            "Lx": load_x,
            "Sy": square_y,
            "Sm": square_mem,
            "Zz": make_dz2,
            "Ih": interleave_w_hid,
            "Ir": interleave_w_rg,
            "I1": interleave_dz1,
            "Hp": hidden_pass,
            "Dz": make_dz1,
            "Qh": lambda k, c: quantize(w_hid_q, E4M3, k, c, held["w_hid", k, c]),
            "Qr": lambda k, c: quantize(w_rg_q, E4M3, k, c, held["w_rg", k, c]),
            "Qz": lambda k, h: quantize(dz2_q, E5M2, k, h, held["dz2", k, h]),
            "Q1": lambda g, h: quantize(dz1_q, E5M2, g, h, held["dz1", g, h]),
            "Qt": lambda h, g: quantize(dz1_t_q, E5M2, h, g, held[("dz1_t", g), h]),
            "Qx": lambda h, n: quantize(x_t_q, E4M3, h, n, held[("x_t", n), h]),
            "Tt": lambda g, h, z: transpose(("dz1_t", g), dz1[g], h, z),
            "Cc": lambda g, h, z, engine: copy_transposed(("dz1_t", g), h, z, engine),
            "Xt": lambda n, h, z: transpose(("x_t", n), held["x_raw", n], h, z),
            "Xc": lambda n, h, z, engine: copy_transposed(("x_t", n), h, z, engine),
            "P0": out_0_product,
            "E0": out_0_copy,
            "W0": out_0_store,
            "P1": out_1_product,
            "E1": out_1_copy,
            "W1": out_1_store,
        }

        nc.vector.memset(minus_half[:], -0.5)
        make_identity(nc, ident[:])

        with tc.manual_schedule():
            for step in ORDER.split():
                arguments = [int(c) if c in "0123" else c for c in step[2:]]
                steps[step[:2]](*arguments)
